import numpy as np
import ml_dtypes


def mxq(x, axis, fmt="e4m3"):
    dtype, down = {"e4m3": (ml_dtypes.float8_e4m3fn, 7), "e5m2": (ml_dtypes.float8_e5m2, 14)}[fmt]
    v = np.moveaxis(np.asarray(x, np.float32).astype(ml_dtypes.bfloat16).astype(np.float64), axis, -1)
    blocks = v.reshape(v.shape[:-1] + (-1, 32))
    amax = np.abs(blocks).max(-1, keepdims=True)
    byte = np.maximum(np.where(amax > 0, np.frexp(amax)[1] - 1 + 127, 0) - down, 1)
    scale = np.exp2(byte - 127.0)
    codes = (blocks / scale).astype(np.float32).astype(dtype).astype(np.float64)
    return np.moveaxis((codes * scale).reshape(v.shape), -1, axis)


WIDE = False


def mx_kscale(k):
    if not WIDE:
        return np.ones(k)
    levels = np.array([10, -10, 5, -5, 0])
    if k % 512:
        return np.exp2(np.random.permutation(np.resize(levels, k // 32))).repeat(32)
    a = np.empty((k // 512, 16))
    for p in range(k // 512):
        a[p, :8] = np.random.permutation(np.resize(levels, 8))
        for g in range(8):
            far = levels[np.abs(levels - a[p, g]) >= 10]
            a[p, g + 8] = far[np.random.randint(len(far))]
    return np.exp2(a.ravel()).repeat(32)


BF16 = ml_dtypes.bfloat16


def bf(x):
    return np.asarray(x, np.float32).astype(BF16)


def f64(x):
    return np.asarray(x).astype(np.float64)


B, S, D, NH, HS, ROT = 2, 512, 1024, 8, 128, 32
BASE = 10000.0
HALF = ROT // 2
W3 = 3 * NH * HS


def rotate_half(x):
    return np.concatenate([-x[..., HALF:], x[..., :HALF]], axis=-1)


def rope_tables():
    inv_freq = 1.0 / BASE ** (np.arange(0, ROT, 2) / ROT)
    freqs = np.outer(np.arange(S), inv_freq)
    emb = np.concatenate([freqs, freqs], axis=-1)
    return np.cos(emb)[None, None], np.sin(emb)[None, None]


def apply_rot(x, cos, sin):
    xr, xp = x[..., :ROT], x[..., ROT:]
    xr = xr * cos + rotate_half(xr) * sin
    return np.concatenate([xr, xp], axis=-1)


def draw0():
    s = mx_kscale(D)
    return {"hidden_states": bf(np.random.standard_normal((B, S, D)) * s),
            "w_qkv": bf(np.random.standard_normal((D, W3)) * 1.5 / np.sqrt(D) / s[:, None])}


def core(hidden_states, w_qkv):
    qkv = mxq(f64(hidden_states), 2, "e4m3") @ mxq(f64(w_qkv), 0, "e4m3")
    qkv = qkv.reshape(B, S, NH, 3 * HS)
    q = qkv[..., :HS].transpose(0, 2, 1, 3)
    k = qkv[..., HS:2 * HS].transpose(0, 2, 1, 3)
    v = qkv[..., 2 * HS:].transpose(0, 2, 1, 3)
    cos, sin = rope_tables()
    return apply_rot(q, cos, sin), apply_rot(k, cos, sin), v


def e4m3fn_bytes(y):
    return np.clip(np.asarray(y, np.float64), -448.0, 448.0).astype(np.float32).astype(ml_dtypes.float8_e4m3fn).view(np.uint8)


def e4m3fn_values(b):
    return np.asarray(b, np.uint8).view(ml_dtypes.float8_e4m3fn).astype(np.float64)


def setup_inputs():
    d = draw0()
    x0 = np.asarray(d['w_qkv']).astype(np.float64)
    s = (np.max(np.abs(x0), axis=(1,), keepdims=True) / 448.0).astype(np.float32)
    out = {}
    for k, v in d.items():
        if k == 'w_qkv':
            out['w_qkv_bytes'] = e4m3fn_bytes(x0 / s.astype(np.float64))
            out['w_qkv_scale'] = s
        else:
            out[k] = v
    return out


def reference(hidden_states, w_qkv_bytes, w_qkv_scale):
    return core(hidden_states, e4m3fn_values(w_qkv_bytes) * w_qkv_scale.astype(np.float64))

@@ -1,0 +1,294 @@
+from contextlib import ExitStack
+
+import concourse.mybir as mybir
+from concourse.masks import make_identity
+
+NB = 2
+SEQ = 512
+DM = 1024
+NH = 8
+HS = 128
+ROT = 32
+BASE = 10000.0
+HALF = ROT // 2
+FLOPS = 2 * NB * SEQ * DM * 3 * NH * HS
+
+F32 = mybir.dt.float32
+BF16 = mybir.dt.bfloat16
+I32 = mybir.dt.int32
+U32 = mybir.dt.uint32
+U8 = mybir.dt.uint8
+FP8 = mybir.dt.float8_e4m3fn
+FP8X4 = mybir.dt.float8_e4m3fn_x4
+ALU = mybir.AluOpType
+ACT = mybir.ActivationFunctionType
+
+P = 128
+CW = 768
+NSTEP = 8
+NHALF = 8
+PI = 3.141592653589793
+TWO_PI_HI = 6.28125
+TWO_PI_LO = 2.0 * PI - TWO_PI_HI
+
+V_PLANES = {0: (2, 3), 1: (3,), 2: (2, 3), 3: (3,), 4: (2, 3), 5: (3,), 6: (2, 3), 7: (3,)}
+S_INTERLEAVE_V = (1, 7)
+V_COPY = {6: (3,), 7: (1, 3)}
+
+
+def tile_gptneoxjapaneseattention_pa_kernel(tc, hidden_states, w_qkv_bytes, w_qkv_scale, out_0, out_1, out_2):
+    nc = tc.nc
+    with ExitStack() as ctx:
+        const = ctx.enter_context(tc.tile_pool(name="const", bufs=1))
+        planes = ctx.enter_context(tc.tile_pool(name="planes", bufs=3))
+        inter = ctx.enter_context(tc.tile_pool(name="inter", bufs=2))
+        outp = ctx.enter_context(tc.tile_pool(name="outp", bufs=3))
+        psum = ctx.enter_context(tc.psum_pool(name="psum", bufs=8))
+
+        sc = const.tile([P, 8], F32, name="sc")
+        nc.sync.dma_start(
+            out=sc[:].rearrange("p (g t) -> p g t", g=2),
+            in_=w_qkv_scale.rearrange("(g p t) o -> p g (t o)", g=2, p=P),
+        )
+        wview = w_qkv_bytes.rearrange("(g p t) n -> g p t n", g=2, p=P)
+        wb = []
+        for w in range(NHALF):
+            wb.append(const.tile([P, 4, CW], U8, name="wb%d" % w))
+        xraw = []
+        for b in range(NB):
+            xraw.append(const.tile([P, 4, DM], BF16, name="xraw%d" % b))
+
+        def load_w(w, pieces):
+            c, g = divmod(w, 2)
+            n = 4 // pieces
+            for i in range(pieces):
+                nc.sync.dma_start(out=wb[w][:, n * i:n * (i + 1), :], in_=wview[g][:, n * i:n * (i + 1), CW * c:CW * (c + 1)])
+
+        def load_x(b):
+            xv = hidden_states[b].rearrange("(p r) k -> p r k", r=4)
+            for hf in range(2):
+                nc.sync.dma_start(out=xraw[b][:, 2 * hf:2 * hf + 2, :], in_=xv[:, 2 * hf:2 * hf + 2, :])
+
+        load_w(0, 2)
+        load_w(1, 2)
+        load_x(0)
+        load_w(2, 1)
+        load_w(3, 1)
+        load_x(1)
+        for w in range(4, NHALF):
+            load_w(w, 1)
+
+        warm = const.tile([P, 2], F32, name="warm")
+        nc.vector.memset(warm[:], 0.0)
+        nc.scalar.activation(out=warm[:, 1:2], in_=warm[:, 0:1], func=ACT.Sin)
+
+        ident = const.tile([P, P], F32, name="ident")
+        make_identity(nc, ident[:])
+
+        xc = const.tile([P, 4, 512], U32, name="xc", align_bytes=64)
+        xs = const.tile([P, 4, 512], U8, name="xs", align_bytes=64)
+        wcqk = const.tile([P, NHALF, 512], U32, name="wcqk", align_bytes=64)
+        wsqk = const.tile([P, NHALF, 512], U8, name="wsqk", align_bytes=64)
+        wcv = const.tile([P, NHALF, 256], U32, name="wcv", align_bytes=64)
+        wsv = const.tile([P, NHALF, 256], U8, name="wsv", align_bytes=64)
+
+        wp = {}
+        wiqk = {}
+        wiv = {}
+
+        def widen(w):
+            g = w % 2
+            wp[w] = planes.tile([P, 4, CW], BF16, name="wp", tag="wp")
+            for t in range(4):
+                j = 4 * g + t
+                src = wb[w][:, t, :].bitcast(FP8)
+                if t in V_PLANES[w]:
+                    nc.vector.tensor_scalar(out=wp[w][:, t, :], in0=src, scalar1=sc[:, j:j + 1], scalar2=None, op0=ALU.mult)
+                else:
+                    nc.scalar.activation(out=wp[w][:, t, :], in_=src, func=ACT.Copy, scale=sc[:, j:j + 1])
+
+        def interleave_qk(w):
+            src = wp[w][:].rearrange("p t (h y f) -> p y h f t", h=2, y=3)
+            wiqk[w] = inter.tile([P, 512, 4], BF16, name="wiqk", tag="wiqk", align_bytes=64)
+            nc.vector.tensor_copy(out=wiqk[w][:].rearrange("p (y h f) t -> p y h f t", y=2, h=2), in_=src[:, 0:2])
+
+        def interleave_v(w):
+            src = wp[w][:].rearrange("p t (h y f) -> p y h f t", h=2, y=3)
+            wiv[w] = inter.tile([P, 256, 4], BF16, name="wiv", tag="wiv", align_bytes=64)
+            if w in S_INTERLEAVE_V:
+                nc.scalar.copy(out=wiv[w][:].rearrange("p (h f) t -> p h f t", h=2), in_=src[:, 2])
+            else:
+                nc.vector.tensor_copy(out=wiv[w][:].rearrange("p (h f) t -> p h f t", h=2), in_=src[:, 2])
+
+        def quant_qk(w):
+            nc.vector.quantize_mx(out=wcqk[:, w, :].bitcast(FP8X4), scales=wsqk[:, w, :], in_=wiqk[w][:].rearrange("p n t -> p (n t)"))
+
+        def quant_v(w):
+            nc.vector.quantize_mx(out=wcv[:, w, :].bitcast(FP8X4), scales=wsv[:, w, :], in_=wiv[w][:].rearrange("p n t -> p (n t)"))
+
+        xg = {}
+
+        def x_turn(b, g):
+            words = xraw[b][:].bitcast(F32)
+            xg[(b, g)] = inter.tile([P, 512, 4], BF16, name="xg", tag="xg", align_bytes=64)
+            xgw = xg[(b, g)][:].rearrange("p n j -> p (n j)").bitcast(F32).rearrange("p (n u) -> p n u", u=2)
+            for rp in range(2):
+                bank = psum.tile([P, 512], F32, name="xt", tag="ps")
+                bv = bank[:].rearrange("p (u n) -> p u n", u=2)
+                for rr in range(2):
+                    for u in range(2):
+                        nc.tensor.transpose(bv[:, u, P * rr:P * (rr + 1)], words[:, 2 * rp + rr, 256 * g + u:256 * (g + 1):2], ident[:])
+                nc.scalar.copy(out=xgw[:, 256 * rp:256 * (rp + 1), :], in_=bv.rearrange("p u n -> p n u"))
+
+        def x_quant(b, g):
+            nc.vector.quantize_mx(out=xc[:, 2 * b + g, :].bitcast(FP8X4), scales=xs[:, 2 * b + g, :], in_=xg[(b, g)][:].rearrange("p n j -> p (n j)"))
+
+        def mm_group(out, b, r, codes, scales, c):
+            for g in range(2):
+                nc.tensor.matmul_mx(
+                    out=out,
+                    lhsT=xc[:, 2 * b + g, P * r:P * (r + 1)].bitcast(FP8X4),
+                    lhsT_scale=xs[:, 2 * b + g, P * r:P * (r + 1)],
+                    rhs=codes[:, 2 * c + g, :].bitcast(FP8X4),
+                    rhs_scale=scales[:, 2 * c + g, :],
+                    start=(g == 0),
+                    stop=(g == 1),
+                )
+
+        def mm(s):
+            c, b = divmod(s, 2)
+            qk = []
+            vb = []
+            for rp in range(2):
+                for rr in range(2):
+                    bank = psum.tile([P, 512], F32, name="qk", tag="ps")
+                    mm_group(bank[:], b, 2 * rp + rr, wcqk, wsqk, c)
+                    qk.append(bank)
+                bank = psum.tile([P, 512], F32, name="vb", tag="ps")
+                bv = bank[:].rearrange("p (a n) -> p a n", a=2)
+                for rr in range(2):
+                    mm_group(bv[:, rr, :], b, 2 * rp + rr, wcv, wsv, c)
+                vb.append(bank)
+            return qk, vb
+
+        widen(0)
+        widen(1)
+        interleave_qk(0)
+        interleave_v(0)
+        x_turn(0, 0)
+        quant_qk(0)
+        quant_v(0)
+        interleave_qk(1)
+        interleave_v(1)
+        x_turn(0, 1)
+        x_quant(0, 0)
+        quant_qk(1)
+        quant_v(1)
+        x_quant(0, 1)
+        widen(2)
+        banks = {0: mm(0)}
+        x_turn(1, 0)
+        x_turn(1, 1)
+        x_quant(1, 0)
+        x_quant(1, 1)
+
+        pos_i = const.tile([P, 4], I32, name="pos_i")
+        nc.gpsimd.iota(pos_i[:], pattern=[[1, 4]], base=0, channel_multiplier=4)
+        pos_f = const.tile([P, 4], F32, name="pos_f")
+        nc.vector.tensor_copy(out=pos_f[:], in_=pos_i[:])
+        ang = const.tile([P, 4, HALF], F32, name="ang")
+        for j in range(HALF):
+            nc.vector.tensor_scalar(out=ang[:, :, j], in0=pos_f[:], scalar1=1.0 / BASE ** (2 * j / ROT), scalar2=None, op0=ALU.mult)
+        arg = const.tile([P, 256], F32, name="arg")
+        arg4 = arg[:].rearrange("p (r q j) -> p r q j", r=4, q=4)
+        for q in range(4):
+            nc.vector.tensor_scalar(out=arg4[:, :, q, :], in0=ang[:], scalar1=(0.5 * PI if q < 2 else 0.0), scalar2=None, op0=ALU.add)
+        turn_i = const.tile([P, 256], I32, name="turn_i")
+        nc.vector.tensor_scalar(out=turn_i[:], in0=arg[:], scalar1=0.5 / PI, scalar2=None, op0=ALU.mult)
+        turn_f = const.tile([P, 256], F32, name="turn_f")
+        nc.vector.tensor_copy(out=turn_f[:], in_=turn_i[:])
+        red1 = const.tile([P, 256], F32, name="red1")
+        nc.vector.scalar_tensor_tensor(out=red1[:], in0=turn_f[:], scalar=-TWO_PI_HI, in1=arg[:], op0=ALU.mult, op1=ALU.add)
+        red2 = const.tile([P, 256], F32, name="red2")
+        nc.vector.scalar_tensor_tensor(out=red2[:], in0=turn_f[:], scalar=-TWO_PI_LO, in1=red1[:], op0=ALU.mult, op1=ALU.add)
+        wrap = const.tile([P, 256], F32, name="wrap")
+        nc.vector.tensor_scalar(out=wrap[:], in0=red2[:], scalar1=PI, scalar2=-2.0 * PI, op0=ALU.is_gt, op1=ALU.mult)
+        red3 = const.tile([P, 256], F32, name="red3")
+        nc.vector.tensor_tensor(out=red3[:], in0=red2[:], in1=wrap[:], op=ALU.add)
+        cs = const.tile([P, 256], F32, name="cs")
+        cs3 = cs[:].rearrange("p (r c) -> p r c", r=4)
+        red33 = red3[:].rearrange("p (r c) -> p r c", r=4)
+        nc.scalar.activation(out=cs3[:, :, 0:48], in_=red33[:, :, 0:48], func=ACT.Sin)
+        nc.scalar.activation(out=cs3[:, :, 48:64], in_=red33[:, :, 48:64], func=ACT.Sin, scale=-1.0)
+        cs5 = cs[:].rearrange("p (r q o c) -> p r q o c", r=4, q=2, o=1)
+
+        for s in range(NSTEP):
+            c, b = divmod(s, 2)
+            qk, vb = banks[s]
+            otqk = outp.tile([P, 4, 4, HS], F32, name="otqk", tag="otqk")
+            otv = outp.tile([P, 2, 4, HS], F32, name="otv", tag="otv")
+            prod = outp.tile([P, 2, 4, 4, ROT], F32, name="prod", tag="prod")
+            last = s == NSTEP - 1
+
+            def rope(r):
+                bv = qk[r][:].rearrange("p (o k f) -> p o k f", o=1, k=4)
+                nc.vector.tensor_tensor(
+                    out=prod[:, :, :, r, :],
+                    in0=bv[:, :, :, 0:ROT].to_broadcast([P, 2, 4, ROT]),
+                    in1=cs5[:, r].to_broadcast([P, 2, 4, ROT]),
+                    op=ALU.mult,
+                )
+                if r in V_COPY.get(s, ()):
+                    nc.vector.tensor_copy(out=otqk[:, :, r, ROT:HS], in_=bv[:, 0, :, ROT:HS])
+                else:
+                    nc.scalar.copy(out=otqk[:, :, r, ROT:HS], in_=bv[:, 0, :, ROT:HS])
+
+            def copy_v(rp):
+                nc.scalar.copy(
+                    out=otv[:, :, 2 * rp:2 * rp + 2, :].rearrange("p h a d -> p a h d"),
+                    in_=vb[rp][:].rearrange("p (a h d) -> p a h d", a=2, h=2),
+                )
+                if last:
+                    nc.sync.dma_start(
+                        out=out_2[b, 2 * c:2 * c + 2].rearrange("h (p r) d -> p h r d", r=4)[:, :, 2 * rp:2 * rp + 2, :].rearrange("p h r d -> p h (r d)"),
+                        in_=otv[:, :, 2 * rp:2 * rp + 2, :].rearrange("p h r d -> p h (r d)"),
+                    )
+
+            def finish(y, dst):
+                nc.vector.tensor_tensor(
+                    out=otqk[:, 2 * y:2 * y + 2, :, 0:ROT].rearrange("p k r (h j) -> p (k r) h j", h=2),
+                    in0=prod[:, 0, 2 * y:2 * y + 2].rearrange("p k r (h j) -> p (k r) h j", h=2),
+                    in1=prod[:, 1, 2 * y:2 * y + 2].rearrange("p k r (h j) -> p (k r) h j", h=2)[:, :, ::-1, :],
+                    op=ALU.add,
+                )
+                nc.sync.dma_start(
+                    out=dst[b, 2 * c:2 * c + 2].rearrange("h (p r) d -> p h (r d)", r=4),
+                    in_=otqk[:, 2 * y:2 * y + 2].rearrange("p k r d -> p k (r d)"),
+                )
+
+            more = s + 2 < NHALF
+            rope(0)
+            if more:
+                interleave_qk(s + 2)
+            rope(1)
+            if more:
+                interleave_v(s + 2)
+            copy_v(0)
+            if more:
+                quant_qk(s + 2)
+            rope(2)
+            if more:
+                quant_v(s + 2)
+            if s + 1 < NSTEP:
+                banks[s + 1] = mm(s + 1)
+            rope(3)
+            finish(0, out_0)
+            copy_v(1)
+            if not last:
+                nc.sync.dma_start(
+                    out=out_2[b, 2 * c:2 * c + 2].rearrange("h (p r) d -> p h (r d)", r=4),
+                    in_=otv[:].rearrange("p h r d -> p h (r d)"),
+                )
+            finish(1, out_1)
+            if s + 3 < NHALF:
+                widen(s + 3)

@@ -33,7 +33,8 @@ TWO_PI_LO = 2.0 * PI - TWO_PI_HI
 
 V_PLANES = {0: (2, 3), 1: (3,), 2: (2, 3), 3: (3,), 4: (2, 3), 5: (3,), 6: (2, 3), 7: (3,)}
 S_INTERLEAVE_V = (1, 7)
-V_COPY = {6: (3,), 7: (1, 3)}
+V_COPY = {7: (1, 3)}
+LATE_V = 6
 
 
 def tile_gptneoxjapaneseattention_pa_kernel(tc, hidden_states, w_qkv_bytes, w_qkv_scale, out_0, out_1, out_2):
@@ -52,8 +53,11 @@ def tile_gptneoxjapaneseattention_pa_kernel(tc, hidden_states, w_qkv_bytes, w_qk
         )
         wview = w_qkv_bytes.rearrange("(g p t) n -> g p t n", g=2, p=P)
         wb = []
-        for w in range(NHALF):
+        for w in range(4):
             wb.append(const.tile([P, 4, CW], U8, name="wb%d" % w))
+        wbl = []
+        for g in range(2):
+            wbl.append(const.tile([P, 4, 2 * CW], U8, name="wbl%d" % g))
         xraw = []
         for b in range(NB):
             xraw.append(const.tile([P, 4, DM], BF16, name="xraw%d" % b))
@@ -75,8 +79,14 @@ def tile_gptneoxjapaneseattention_pa_kernel(tc, hidden_states, w_qkv_bytes, w_qk
         load_w(2, 1)
         load_w(3, 1)
         load_x(1)
-        for w in range(4, NHALF):
-            load_w(w, 1)
+        for g in range(2):
+            nc.sync.dma_start(out=wbl[g][:], in_=wview[g][:, :, 2 * CW:4 * CW])
+
+        def wbytes(w, t):
+            c, g = divmod(w, 2)
+            if c < 2:
+                return wb[w][:, t, :]
+            return wbl[g][:, t, CW * (c - 2):CW * (c - 1)]
 
         warm = const.tile([P, 2], F32, name="warm")
         nc.vector.memset(warm[:], 0.0)
@@ -101,7 +111,7 @@ def tile_gptneoxjapaneseattention_pa_kernel(tc, hidden_states, w_qkv_bytes, w_qk
             wp[w] = planes.tile([P, 4, CW], BF16, name="wp", tag="wp")
             for t in range(4):
                 j = 4 * g + t
-                src = wb[w][:, t, :].bitcast(FP8)
+                src = wbytes(w, t).bitcast(FP8)
                 if t in V_PLANES[w]:
                     nc.vector.tensor_scalar(out=wp[w][:, t, :], in0=src, scalar1=sc[:, j:j + 1], scalar2=None, op0=ALU.mult)
                 else:
@@ -155,21 +165,29 @@ def tile_gptneoxjapaneseattention_pa_kernel(tc, hidden_states, w_qkv_bytes, w_qk
                     stop=(g == 1),
                 )
 
-        def mm(s):
+        qkb = {}
+        vbb = {}
+
+        def mm_qk(s, rp):
             c, b = divmod(s, 2)
-            qk = []
-            vb = []
+            for rr in range(2):
+                bank = psum.tile([P, 512], F32, name="qk", tag="ps")
+                mm_group(bank[:], b, 2 * rp + rr, wcqk, wsqk, c)
+                qkb[(s, 2 * rp + rr)] = bank
+
+        def mm_v(s, rp):
+            c, b = divmod(s, 2)
+            bank = psum.tile([P, 512], F32, name="vb", tag="ps")
+            bv = bank[:].rearrange("p (a n) -> p a n", a=2)
+            for rr in range(2):
+                mm_group(bv[:, rr, :], b, 2 * rp + rr, wcv, wsv, c)
+            vbb[(s, rp)] = bank
+
+        def mm(s):
             for rp in range(2):
-                for rr in range(2):
-                    bank = psum.tile([P, 512], F32, name="qk", tag="ps")
-                    mm_group(bank[:], b, 2 * rp + rr, wcqk, wsqk, c)
-                    qk.append(bank)
-                bank = psum.tile([P, 512], F32, name="vb", tag="ps")
-                bv = bank[:].rearrange("p (a n) -> p a n", a=2)
-                for rr in range(2):
-                    mm_group(bv[:, rr, :], b, 2 * rp + rr, wcv, wsv, c)
-                vb.append(bank)
-            return qk, vb
+                mm_qk(s, rp)
+                if s < LATE_V:
+                    mm_v(s, rp)
 
         widen(0)
         widen(1)
@@ -186,7 +204,7 @@ def tile_gptneoxjapaneseattention_pa_kernel(tc, hidden_states, w_qkv_bytes, w_qk
         quant_v(1)
         x_quant(0, 1)
         widen(2)
-        banks = {0: mm(0)}
+        mm(0)
         x_turn(1, 0)
         x_turn(1, 1)
         x_quant(1, 0)
@@ -222,16 +240,37 @@ def tile_gptneoxjapaneseattention_pa_kernel(tc, hidden_states, w_qkv_bytes, w_qk
         nc.scalar.activation(out=cs3[:, :, 48:64], in_=red33[:, :, 48:64], func=ACT.Sin, scale=-1.0)
         cs5 = cs[:].rearrange("p (r q o c) -> p r q o c", r=4, q=2, o=1)
 
+        otvs = {}
+
+        def copy_v(s, rp, engine, split):
+            c, b = divmod(s, 2)
+            if rp == 0:
+                otvs[s] = outp.tile([P, 2, 4, HS], F32, name="otv", tag="otv")
+            otv = otvs[s]
+            dst = otv[:, :, 2 * rp:2 * rp + 2, :].rearrange("p h a d -> p a h d")
+            src = vbb[(s, rp)][:].rearrange("p (a h d) -> p a h d", a=2, h=2)
+            if engine == "v":
+                nc.vector.tensor_copy(out=dst, in_=src)
+            else:
+                nc.scalar.copy(out=dst, in_=src)
+            if split:
+                nc.sync.dma_start(
+                    out=out_2[b, 2 * c:2 * c + 2].rearrange("h (p r) d -> p h r d", r=4)[:, :, 2 * rp:2 * rp + 2, :].rearrange("p h r d -> p h (r d)"),
+                    in_=otv[:, :, 2 * rp:2 * rp + 2, :].rearrange("p h r d -> p h (r d)"),
+                )
+            elif rp == 1:
+                nc.sync.dma_start(
+                    out=out_2[b, 2 * c:2 * c + 2].rearrange("h (p r) d -> p h (r d)", r=4),
+                    in_=otv[:].rearrange("p h r d -> p h (r d)"),
+                )
+
         for s in range(NSTEP):
             c, b = divmod(s, 2)
-            qk, vb = banks[s]
             otqk = outp.tile([P, 4, 4, HS], F32, name="otqk", tag="otqk")
-            otv = outp.tile([P, 2, 4, HS], F32, name="otv", tag="otv")
             prod = outp.tile([P, 2, 4, 4, ROT], F32, name="prod", tag="prod")
-            last = s == NSTEP - 1
 
             def rope(r):
-                bv = qk[r][:].rearrange("p (o k f) -> p o k f", o=1, k=4)
+                bv = qkb[(s, r)][:].rearrange("p (o k f) -> p o k f", o=1, k=4)
                 nc.vector.tensor_tensor(
                     out=prod[:, :, :, r, :],
                     in0=bv[:, :, :, 0:ROT].to_broadcast([P, 2, 4, ROT]),
@@ -242,17 +281,6 @@ def tile_gptneoxjapaneseattention_pa_kernel(tc, hidden_states, w_qkv_bytes, w_qk
                     nc.vector.tensor_copy(out=otqk[:, :, r, ROT:HS], in_=bv[:, 0, :, ROT:HS])
                 else:
                     nc.scalar.copy(out=otqk[:, :, r, ROT:HS], in_=bv[:, 0, :, ROT:HS])
-
-            def copy_v(rp):
-                nc.scalar.copy(
-                    out=otv[:, :, 2 * rp:2 * rp + 2, :].rearrange("p h a d -> p a h d"),
-                    in_=vb[rp][:].rearrange("p (a h d) -> p a h d", a=2, h=2),
-                )
-                if last:
-                    nc.sync.dma_start(
-                        out=out_2[b, 2 * c:2 * c + 2].rearrange("h (p r) d -> p h r d", r=4)[:, :, 2 * rp:2 * rp + 2, :].rearrange("p h r d -> p h (r d)"),
-                        in_=otv[:, :, 2 * rp:2 * rp + 2, :].rearrange("p h r d -> p h (r d)"),
-                    )
 
             def finish(y, dst):
                 nc.vector.tensor_tensor(
@@ -266,29 +294,44 @@ def tile_gptneoxjapaneseattention_pa_kernel(tc, hidden_states, w_qkv_bytes, w_qk
                     in_=otqk[:, 2 * y:2 * y + 2].rearrange("p k r d -> p k (r d)"),
                 )
 
-            more = s + 2 < NHALF
+            w = s + 2
+            more = w < NHALF
+            early_v = more and w < LATE_V
             rope(0)
             if more:
-                interleave_qk(s + 2)
+                interleave_qk(w)
+            if s == LATE_V:
+                interleave_v(LATE_V)
             rope(1)
+            if early_v:
+                interleave_v(w)
+            if s == LATE_V:
+                interleave_v(LATE_V + 1)
+            if s < LATE_V:
+                copy_v(s, 0, "s", False)
             if more:
-                interleave_v(s + 2)
-            copy_v(0)
-            if more:
-                quant_qk(s + 2)
+                quant_qk(w)
+            if s == LATE_V:
+                quant_v(LATE_V)
             rope(2)
-            if more:
-                quant_v(s + 2)
+            if early_v:
+                quant_v(w)
+            if s == LATE_V:
+                quant_v(LATE_V + 1)
             if s + 1 < NSTEP:
-                banks[s + 1] = mm(s + 1)
+                mm(s + 1)
             rope(3)
             finish(0, out_0)
-            copy_v(1)
-            if not last:
-                nc.sync.dma_start(
-                    out=out_2[b, 2 * c:2 * c + 2].rearrange("h (p r) d -> p h (r d)", r=4),
-                    in_=otv[:].rearrange("p h r d -> p h (r d)"),
-                )
+            if s < LATE_V:
+                copy_v(s, 1, "s", False)
             finish(1, out_1)
             if s + 3 < NHALF:
                 widen(s + 3)
+
+        for s in range(LATE_V, NSTEP):
+            for rp in range(2):
+                mm_v(s, rp)
+        copy_v(LATE_V, 0, "s", False)
+        copy_v(LATE_V, 1, "v", False)
+        copy_v(LATE_V + 1, 0, "s", True)
+        copy_v(LATE_V + 1, 1, "v", True)

@@ -118,17 +118,21 @@ def tile_gptneoxjapaneseattention_pa_kernel(tc, hidden_states, w_qkv_bytes, w_qk
                     nc.scalar.activation(out=wp[w][:, t, :], in_=src, func=ACT.Copy, scale=sc[:, j:j + 1])
 
         def interleave_qk(w):
-            src = wp[w][:].rearrange("p t (h y f) -> p y h f t", h=2, y=3)
+            src = wp[w][:].rearrange("p t (h y c i) -> p y h c t i", h=2, y=3, i=4)
             wiqk[w] = inter.tile([P, 512, 4], BF16, name="wiqk", tag="wiqk", align_bytes=64)
-            nc.vector.tensor_copy(out=wiqk[w][:].rearrange("p (y h f) t -> p y h f t", y=2, h=2), in_=src[:, 0:2])
+            dst = wiqk[w][:].rearrange("p (y h c i) t -> p y h c t i", y=2, h=2, i=4)
+            for y in range(2):
+                nc.vector.tensor_copy(out=dst[:, y], in_=src[:, y])
 
         def interleave_v(w):
-            src = wp[w][:].rearrange("p t (h y f) -> p y h f t", h=2, y=3)
+            src = wp[w][:].rearrange("p t (h y c i) -> p y h c t i", h=2, y=3, i=4)
             wiv[w] = inter.tile([P, 256, 4], BF16, name="wiv", tag="wiv", align_bytes=64)
+            dst = wiv[w][:].rearrange("p (h c i) t -> p h c t i", h=2, i=4)
             if w in S_INTERLEAVE_V:
-                nc.scalar.copy(out=wiv[w][:].rearrange("p (h f) t -> p h f t", h=2), in_=src[:, 2])
+                for h in range(2):
+                    nc.scalar.copy(out=dst[:, h], in_=src[:, 2, h])
             else:
-                nc.vector.tensor_copy(out=wiv[w][:].rearrange("p (h f) t -> p h f t", h=2), in_=src[:, 2])
+                nc.vector.tensor_copy(out=dst, in_=src[:, 2])
 
         def quant_qk(w):
             nc.vector.quantize_mx(out=wcqk[:, w, :].bitcast(FP8X4), scales=wsqk[:, w, :], in_=wiqk[w][:].rearrange("p n t -> p (n t)"))
@@ -316,17 +320,17 @@ def tile_gptneoxjapaneseattention_pa_kernel(tc, hidden_states, w_qkv_bytes, w_qk
             rope(2)
             if early_v:
                 quant_v(w)
-            if s == LATE_V:
-                quant_v(LATE_V + 1)
             if s + 1 < NSTEP:
                 mm(s + 1)
             rope(3)
+            if s == LATE_V:
+                quant_v(LATE_V + 1)
+            if s + 3 < NHALF:
+                widen(s + 3)
             finish(0, out_0)
             if s < LATE_V:
                 copy_v(s, 1, "s", False)
             finish(1, out_1)
-            if s + 3 < NHALF:
-                widen(s + 3)
 
         for s in range(LATE_V, NSTEP):
             for rp in range(2):

@@ -31,7 +31,7 @@ PI = 3.141592653589793
 TWO_PI_HI = 6.28125
 TWO_PI_LO = 2.0 * PI - TWO_PI_HI
 
-V_PLANES = {0: (2, 3), 1: (3,), 2: (2, 3), 3: (3,), 4: (2, 3), 5: (3,), 6: (2, 3), 7: (3,)}
+V_PLANES = {0: (2, 3), 1: (3,), 2: (2, 3), 3: (2, 3), 4: (2, 3), 5: (2, 3), 6: (2, 3), 7: (3,)}
 S_INTERLEAVE_V = (1, 7)
 V_COPY = {7: (1, 3)}
 LATE_V = 6
@@ -91,6 +91,28 @@ def tile_gptneoxjapaneseattention_pa_kernel(tc, hidden_states, w_qkv_bytes, w_qk
         warm = const.tile([P, 2], F32, name="warm")
         nc.vector.memset(warm[:], 0.0)
         nc.scalar.activation(out=warm[:, 1:2], in_=warm[:, 0:1], func=ACT.Sin)
+
+        pos_i = const.tile([P, 4], I32, name="pos_i")
+        nc.gpsimd.iota(pos_i[:], pattern=[[1, 4]], base=0, channel_multiplier=4)
+        pos_f = const.tile([P, 4], F32, name="pos_f")
+        nc.vector.tensor_copy(out=pos_f[:], in_=pos_i[:])
+        arg = const.tile([P, 128], F32, name="arg")
+        arg4 = arg[:].rearrange("p (r q j) -> p r q j", r=4, q=2)
+        for j in range(HALF):
+            nc.vector.tensor_scalar(out=arg4[:, :, 1, j], in0=pos_f[:], scalar1=1.0 / BASE ** (2 * j / ROT), scalar2=None, op0=ALU.mult)
+        nc.vector.tensor_scalar(out=arg4[:, :, 0, :], in0=arg4[:, :, 1, :], scalar1=0.5 * PI, scalar2=None, op0=ALU.add)
+        turn_i = const.tile([P, 128], I32, name="turn_i")
+        nc.vector.tensor_scalar(out=turn_i[:], in0=arg[:], scalar1=0.5 / PI, scalar2=None, op0=ALU.mult)
+        turn_f = const.tile([P, 128], F32, name="turn_f")
+        nc.vector.tensor_copy(out=turn_f[:], in_=turn_i[:])
+        red1 = const.tile([P, 128], F32, name="red1")
+        nc.vector.scalar_tensor_tensor(out=red1[:], in0=turn_f[:], scalar=-TWO_PI_HI, in1=arg[:], op0=ALU.mult, op1=ALU.add)
+        red2 = const.tile([P, 128], F32, name="red2")
+        nc.vector.scalar_tensor_tensor(out=red2[:], in0=turn_f[:], scalar=-TWO_PI_LO, in1=red1[:], op0=ALU.mult, op1=ALU.add)
+        wrap = const.tile([P, 128], F32, name="wrap")
+        nc.vector.tensor_scalar(out=wrap[:], in0=red2[:], scalar1=PI, scalar2=-2.0 * PI, op0=ALU.is_gt, op1=ALU.mult)
+        red3 = const.tile([P, 128], F32, name="red3")
+        nc.vector.tensor_tensor(out=red3[:], in0=red2[:], in1=wrap[:], op=ALU.add)
 
         ident = const.tile([P, P], F32, name="ident")
         make_identity(nc, ident[:])
@@ -195,54 +217,29 @@ def tile_gptneoxjapaneseattention_pa_kernel(tc, hidden_states, w_qkv_bytes, w_qk
 
         widen(0)
         widen(1)
+        cs = const.tile([P, 256], F32, name="cs")
+        cs4 = cs[:].rearrange("p (r q j) -> p r q j", r=4, q=4)
+        red4 = red3[:].rearrange("p (r q j) -> p r q j", r=4, q=2)
+        nc.scalar.activation(out=cs4[:, :, 1:3, :], in_=red4, func=ACT.Sin)
+        nc.scalar.activation(out=cs4[:, :, 0, :], in_=red4[:, :, 0, :], func=ACT.Sin)
+        nc.scalar.activation(out=cs4[:, :, 3, :], in_=red4[:, :, 1, :], func=ACT.Sin, scale=-1.0)
+        cs5 = cs[:].rearrange("p (r q o c) -> p r q o c", r=4, q=2, o=1)
         interleave_qk(0)
-        interleave_v(0)
         x_turn(0, 0)
         quant_qk(0)
-        quant_v(0)
         interleave_qk(1)
-        interleave_v(1)
         x_turn(0, 1)
         x_quant(0, 0)
         quant_qk(1)
-        quant_v(1)
         x_quant(0, 1)
-        widen(2)
-        mm(0)
-        x_turn(1, 0)
-        x_turn(1, 1)
-        x_quant(1, 0)
-        x_quant(1, 1)
-
-        pos_i = const.tile([P, 4], I32, name="pos_i")
-        nc.gpsimd.iota(pos_i[:], pattern=[[1, 4]], base=0, channel_multiplier=4)
-        pos_f = const.tile([P, 4], F32, name="pos_f")
-        nc.vector.tensor_copy(out=pos_f[:], in_=pos_i[:])
-        ang = const.tile([P, 4, HALF], F32, name="ang")
-        for j in range(HALF):
-            nc.vector.tensor_scalar(out=ang[:, :, j], in0=pos_f[:], scalar1=1.0 / BASE ** (2 * j / ROT), scalar2=None, op0=ALU.mult)
-        arg = const.tile([P, 256], F32, name="arg")
-        arg4 = arg[:].rearrange("p (r q j) -> p r q j", r=4, q=4)
-        for q in range(4):
-            nc.vector.tensor_scalar(out=arg4[:, :, q, :], in0=ang[:], scalar1=(0.5 * PI if q < 2 else 0.0), scalar2=None, op0=ALU.add)
-        turn_i = const.tile([P, 256], I32, name="turn_i")
-        nc.vector.tensor_scalar(out=turn_i[:], in0=arg[:], scalar1=0.5 / PI, scalar2=None, op0=ALU.mult)
-        turn_f = const.tile([P, 256], F32, name="turn_f")
-        nc.vector.tensor_copy(out=turn_f[:], in_=turn_i[:])
-        red1 = const.tile([P, 256], F32, name="red1")
-        nc.vector.scalar_tensor_tensor(out=red1[:], in0=turn_f[:], scalar=-TWO_PI_HI, in1=arg[:], op0=ALU.mult, op1=ALU.add)
-        red2 = const.tile([P, 256], F32, name="red2")
-        nc.vector.scalar_tensor_tensor(out=red2[:], in0=turn_f[:], scalar=-TWO_PI_LO, in1=red1[:], op0=ALU.mult, op1=ALU.add)
-        wrap = const.tile([P, 256], F32, name="wrap")
-        nc.vector.tensor_scalar(out=wrap[:], in0=red2[:], scalar1=PI, scalar2=-2.0 * PI, op0=ALU.is_gt, op1=ALU.mult)
-        red3 = const.tile([P, 256], F32, name="red3")
-        nc.vector.tensor_tensor(out=red3[:], in0=red2[:], in1=wrap[:], op=ALU.add)
-        cs = const.tile([P, 256], F32, name="cs")
-        cs3 = cs[:].rearrange("p (r c) -> p r c", r=4)
-        red33 = red3[:].rearrange("p (r c) -> p r c", r=4)
-        nc.scalar.activation(out=cs3[:, :, 0:48], in_=red33[:, :, 0:48], func=ACT.Sin)
-        nc.scalar.activation(out=cs3[:, :, 48:64], in_=red33[:, :, 48:64], func=ACT.Sin, scale=-1.0)
-        cs5 = cs[:].rearrange("p (r q o c) -> p r q o c", r=4, q=2, o=1)
+        mm_qk(0, 0)
+        mm_qk(0, 1)
+        interleave_v(0)
+        interleave_v(1)
+        quant_v(0)
+        quant_v(1)
+        mm_v(0, 0)
+        mm_v(0, 1)
 
         otvs = {}
 
@@ -298,6 +295,27 @@ def tile_gptneoxjapaneseattention_pa_kernel(tc, hidden_states, w_qkv_bytes, w_qk
                     in_=otqk[:, 2 * y:2 * y + 2].rearrange("p k r d -> p k (r d)"),
                 )
 
+            if s == 0:
+                x_turn(1, 0)
+                rope(0)
+                x_turn(1, 1)
+                rope(1)
+                x_quant(1, 0)
+                copy_v(0, 0, "s", False)
+                rope(2)
+                x_quant(1, 1)
+                mm(1)
+                rope(3)
+                widen(2)
+                finish(0, out_0)
+                copy_v(0, 1, "s", False)
+                finish(1, out_1)
+                interleave_qk(2)
+                interleave_v(2)
+                widen(3)
+                quant_qk(2)
+                quant_v(2)
+                continue
             w = s + 2
             more = w < NHALF
             early_v = more and w < LATE_V

@@ -31,7 +31,7 @@ PI = 3.141592653589793
 TWO_PI_HI = 6.28125
 TWO_PI_LO = 2.0 * PI - TWO_PI_HI
 
-V_PLANES = {0: (2, 3), 1: (3,), 2: (2, 3), 3: (2, 3), 4: (2, 3), 5: (2, 3), 6: (2, 3), 7: (3,)}
+V_PLANES = {0: (2, 3), 1: (3,), 2: (2, 3), 3: (3,), 4: (2, 3), 5: (3,), 6: (2, 3), 7: (3,)}
 S_INTERLEAVE_V = (1, 7)
 V_COPY = {7: (1, 3)}
 LATE_V = 6

@@ -32,6 +32,7 @@ TWO_PI_HI = 6.28125
 TWO_PI_LO = 2.0 * PI - TWO_PI_HI
 
 V_PLANES = {0: (2, 3), 1: (3,), 2: (2, 3), 3: (3,), 4: (2, 3), 5: (3,), 6: (2, 3), 7: (3,)}
+SHARED_PLANE = (3, 2)
 S_INTERLEAVE_V = (1, 7)
 V_COPY = {7: (1, 3)}
 LATE_V = 6
@@ -134,7 +135,10 @@ def tile_gptneoxjapaneseattention_pa_kernel(tc, hidden_states, w_qkv_bytes, w_qk
             for t in range(4):
                 j = 4 * g + t
                 src = wbytes(w, t).bitcast(FP8)
-                if t in V_PLANES[w]:
+                if (w, t) == SHARED_PLANE:
+                    nc.vector.tensor_scalar(out=wp[w][:, t, 0:CW // 2], in0=src[:, 0:CW // 2], scalar1=sc[:, j:j + 1], scalar2=None, op0=ALU.mult)
+                    nc.scalar.activation(out=wp[w][:, t, CW // 2:CW], in_=src[:, CW // 2:CW], func=ACT.Copy, scale=sc[:, j:j + 1])
+                elif t in V_PLANES[w]:
                     nc.vector.tensor_scalar(out=wp[w][:, t, :], in0=src, scalar1=sc[:, j:j + 1], scalar2=None, op0=ALU.mult)
                 else:
                     nc.scalar.activation(out=wp[w][:, t, :], in_=src, func=ACT.Copy, scale=sc[:, j:j + 1])

@@ -287,17 +287,18 @@ def tile_gptneoxjapaneseattention_pa_kernel(tc, hidden_states, w_qkv_bytes, w_qk
                 else:
                     nc.scalar.copy(out=otqk[:, :, r, ROT:HS], in_=bv[:, 0, :, ROT:HS])
 
-            def finish(y, dst):
+            def finish():
                 nc.vector.tensor_tensor(
-                    out=otqk[:, 2 * y:2 * y + 2, :, 0:ROT].rearrange("p k r (h j) -> p (k r) h j", h=2),
-                    in0=prod[:, 0, 2 * y:2 * y + 2].rearrange("p k r (h j) -> p (k r) h j", h=2),
-                    in1=prod[:, 1, 2 * y:2 * y + 2].rearrange("p k r (h j) -> p (k r) h j", h=2)[:, :, ::-1, :],
+                    out=otqk[:, :, :, 0:ROT].rearrange("p k r (h j) -> p (k r) h j", h=2),
+                    in0=prod[:, 0].rearrange("p k r (h j) -> p (k r) h j", h=2),
+                    in1=prod[:, 1].rearrange("p k r (h j) -> p (k r) h j", h=2)[:, :, ::-1, :],
                     op=ALU.add,
                 )
-                nc.sync.dma_start(
-                    out=dst[b, 2 * c:2 * c + 2].rearrange("h (p r) d -> p h (r d)", r=4),
-                    in_=otqk[:, 2 * y:2 * y + 2].rearrange("p k r d -> p k (r d)"),
-                )
+                for y in range(2):
+                    nc.sync.dma_start(
+                        out=(out_0, out_1)[y][b, 2 * c:2 * c + 2].rearrange("h (p r) d -> p h (r d)", r=4),
+                        in_=otqk[:, 2 * y:2 * y + 2].rearrange("p k r d -> p k (r d)"),
+                    )
 
             if s == 0:
                 x_turn(1, 0)
@@ -311,9 +312,8 @@ def tile_gptneoxjapaneseattention_pa_kernel(tc, hidden_states, w_qkv_bytes, w_qk
                 mm(1)
                 rope(3)
                 widen(2)
-                finish(0, out_0)
+                finish()
                 copy_v(0, 1, "s", False)
-                finish(1, out_1)
                 interleave_qk(2)
                 interleave_v(2)
                 widen(3)
@@ -349,10 +349,9 @@ def tile_gptneoxjapaneseattention_pa_kernel(tc, hidden_states, w_qkv_bytes, w_qk
                 quant_v(LATE_V + 1)
             if s + 3 < NHALF:
                 widen(s + 3)
-            finish(0, out_0)
+            finish()
             if s < LATE_V:
                 copy_v(s, 1, "s", False)
-            finish(1, out_1)
 
         for s in range(LATE_V, NSTEP):
             for rp in range(2):

from contextlib import ExitStack

import concourse.mybir as mybir
from concourse.masks import make_identity

NB = 2
SEQ = 512
DM = 1024
NH = 8
HS = 128
ROT = 32
BASE = 10000.0
HALF = ROT // 2
FLOPS = 2 * NB * SEQ * DM * 3 * NH * HS

F32 = mybir.dt.float32
BF16 = mybir.dt.bfloat16
I32 = mybir.dt.int32
U32 = mybir.dt.uint32
U8 = mybir.dt.uint8
FP8 = mybir.dt.float8_e4m3fn
FP8X4 = mybir.dt.float8_e4m3fn_x4
ALU = mybir.AluOpType
ACT = mybir.ActivationFunctionType

P = 128
CW = 768
NSTEP = 8
NHALF = 8
PI = 3.141592653589793
TWO_PI_HI = 6.28125
TWO_PI_LO = 2.0 * PI - TWO_PI_HI

V_PLANES = {0: (2, 3), 1: (3,), 2: (2, 3), 3: (3,), 4: (2, 3), 5: (3,), 6: (2, 3), 7: (3,)}
SHARED_PLANE = (3, 2)
S_INTERLEAVE_V = (1, 7)
V_COPY = {7: (1, 3)}
LATE_V = 6


def tile_gptneoxjapaneseattention_pa_kernel(tc, hidden_states, w_qkv_bytes, w_qkv_scale, out_0, out_1, out_2):
    nc = tc.nc
    with ExitStack() as ctx:
        const = ctx.enter_context(tc.tile_pool(name="const", bufs=1))
        planes = ctx.enter_context(tc.tile_pool(name="planes", bufs=3))
        inter = ctx.enter_context(tc.tile_pool(name="inter", bufs=2))
        outp = ctx.enter_context(tc.tile_pool(name="outp", bufs=3))
        psum = ctx.enter_context(tc.psum_pool(name="psum", bufs=8))

        sc = const.tile([P, 8], F32, name="sc")
        nc.sync.dma_start(
            out=sc[:].rearrange("p (g t) -> p g t", g=2),
            in_=w_qkv_scale.rearrange("(g p t) o -> p g (t o)", g=2, p=P),
        )
        wview = w_qkv_bytes.rearrange("(g p t) n -> g p t n", g=2, p=P)
        wb = []
        for w in range(4):
            wb.append(const.tile([P, 4, CW], U8, name="wb%d" % w))
        wbl = []
        for g in range(2):
            wbl.append(const.tile([P, 4, 2 * CW], U8, name="wbl%d" % g))
        xraw = []
        for b in range(NB):
            xraw.append(const.tile([P, 4, DM], BF16, name="xraw%d" % b))

        def load_w(w, pieces):
            c, g = divmod(w, 2)
            n = 4 // pieces
            for i in range(pieces):
                nc.sync.dma_start(out=wb[w][:, n * i:n * (i + 1), :], in_=wview[g][:, n * i:n * (i + 1), CW * c:CW * (c + 1)])

        def load_x(b):
            xv = hidden_states[b].rearrange("(p r) k -> p r k", r=4)
            for hf in range(2):
                nc.sync.dma_start(out=xraw[b][:, 2 * hf:2 * hf + 2, :], in_=xv[:, 2 * hf:2 * hf + 2, :])

        load_w(0, 2)
        load_w(1, 2)
        load_x(0)
        load_w(2, 1)
        load_w(3, 1)
        load_x(1)
        for g in range(2):
            nc.sync.dma_start(out=wbl[g][:], in_=wview[g][:, :, 2 * CW:4 * CW])

        def wbytes(w, t):
            c, g = divmod(w, 2)
            if c < 2:
                return wb[w][:, t, :]
            return wbl[g][:, t, CW * (c - 2):CW * (c - 1)]

        warm = const.tile([P, 2], F32, name="warm")
        nc.vector.memset(warm[:], 0.0)
        nc.scalar.activation(out=warm[:, 1:2], in_=warm[:, 0:1], func=ACT.Sin)

        pos_i = const.tile([P, 4], I32, name="pos_i")
        nc.gpsimd.iota(pos_i[:], pattern=[[1, 4]], base=0, channel_multiplier=4)
        pos_f = const.tile([P, 4], F32, name="pos_f")
        nc.vector.tensor_copy(out=pos_f[:], in_=pos_i[:])
        arg = const.tile([P, 128], F32, name="arg")
        arg4 = arg[:].rearrange("p (r q j) -> p r q j", r=4, q=2)
        for j in range(HALF):
            nc.vector.tensor_scalar(out=arg4[:, :, 1, j], in0=pos_f[:], scalar1=1.0 / BASE ** (2 * j / ROT), scalar2=None, op0=ALU.mult)
        nc.vector.tensor_scalar(out=arg4[:, :, 0, :], in0=arg4[:, :, 1, :], scalar1=0.5 * PI, scalar2=None, op0=ALU.add)
        turn_i = const.tile([P, 128], I32, name="turn_i")
        nc.vector.tensor_scalar(out=turn_i[:], in0=arg[:], scalar1=0.5 / PI, scalar2=None, op0=ALU.mult)
        turn_f = const.tile([P, 128], F32, name="turn_f")
        nc.vector.tensor_copy(out=turn_f[:], in_=turn_i[:])
        red1 = const.tile([P, 128], F32, name="red1")
        nc.vector.scalar_tensor_tensor(out=red1[:], in0=turn_f[:], scalar=-TWO_PI_HI, in1=arg[:], op0=ALU.mult, op1=ALU.add)
        red2 = const.tile([P, 128], F32, name="red2")
        nc.vector.scalar_tensor_tensor(out=red2[:], in0=turn_f[:], scalar=-TWO_PI_LO, in1=red1[:], op0=ALU.mult, op1=ALU.add)
        wrap = const.tile([P, 128], F32, name="wrap")
        nc.vector.tensor_scalar(out=wrap[:], in0=red2[:], scalar1=PI, scalar2=-2.0 * PI, op0=ALU.is_gt, op1=ALU.mult)
        red3 = const.tile([P, 128], F32, name="red3")
        nc.vector.tensor_tensor(out=red3[:], in0=red2[:], in1=wrap[:], op=ALU.add)

        ident = const.tile([P, P], F32, name="ident")
        make_identity(nc, ident[:])

        xc = const.tile([P, 4, 512], U32, name="xc", align_bytes=64)
        xs = const.tile([P, 4, 512], U8, name="xs", align_bytes=64)
        wcqk = const.tile([P, NHALF, 512], U32, name="wcqk", align_bytes=64)
        wsqk = const.tile([P, NHALF, 512], U8, name="wsqk", align_bytes=64)
        wcv = const.tile([P, NHALF, 256], U32, name="wcv", align_bytes=64)
        wsv = const.tile([P, NHALF, 256], U8, name="wsv", align_bytes=64)

        wp = {}
        wiqk = {}
        wiv = {}

        def widen(w):
            g = w % 2
            wp[w] = planes.tile([P, 4, CW], BF16, name="wp", tag="wp")
            for t in range(4):
                j = 4 * g + t
                src = wbytes(w, t).bitcast(FP8)
                if (w, t) == SHARED_PLANE:
                    nc.vector.tensor_scalar(out=wp[w][:, t, 0:CW // 2], in0=src[:, 0:CW // 2], scalar1=sc[:, j:j + 1], scalar2=None, op0=ALU.mult)
                    nc.scalar.activation(out=wp[w][:, t, CW // 2:CW], in_=src[:, CW // 2:CW], func=ACT.Copy, scale=sc[:, j:j + 1])
                elif t in V_PLANES[w]:
                    nc.vector.tensor_scalar(out=wp[w][:, t, :], in0=src, scalar1=sc[:, j:j + 1], scalar2=None, op0=ALU.mult)
                else:
                    nc.scalar.activation(out=wp[w][:, t, :], in_=src, func=ACT.Copy, scale=sc[:, j:j + 1])

        def interleave_qk(w):
            src = wp[w][:].rearrange("p t (h y c i) -> p y h c t i", h=2, y=3, i=4)
            wiqk[w] = inter.tile([P, 512, 4], BF16, name="wiqk", tag="wiqk", align_bytes=64)
            dst = wiqk[w][:].rearrange("p (y h c i) t -> p y h c t i", y=2, h=2, i=4)
            for y in range(2):
                nc.vector.tensor_copy(out=dst[:, y], in_=src[:, y])

        def interleave_v(w):
            src = wp[w][:].rearrange("p t (h y c i) -> p y h c t i", h=2, y=3, i=4)
            wiv[w] = inter.tile([P, 256, 4], BF16, name="wiv", tag="wiv", align_bytes=64)
            dst = wiv[w][:].rearrange("p (h c i) t -> p h c t i", h=2, i=4)
            if w in S_INTERLEAVE_V:
                for h in range(2):
                    nc.scalar.copy(out=dst[:, h], in_=src[:, 2, h])
            else:
                nc.vector.tensor_copy(out=dst, in_=src[:, 2])

        def quant_qk(w):
            nc.vector.quantize_mx(out=wcqk[:, w, :].bitcast(FP8X4), scales=wsqk[:, w, :], in_=wiqk[w][:].rearrange("p n t -> p (n t)"))

        def quant_v(w):
            nc.vector.quantize_mx(out=wcv[:, w, :].bitcast(FP8X4), scales=wsv[:, w, :], in_=wiv[w][:].rearrange("p n t -> p (n t)"))

        xg = {}

        def x_turn(b, g):
            words = xraw[b][:].bitcast(F32)
            xg[(b, g)] = inter.tile([P, 512, 4], BF16, name="xg", tag="xg", align_bytes=64)
            xgw = xg[(b, g)][:].rearrange("p n j -> p (n j)").bitcast(F32).rearrange("p (n u) -> p n u", u=2)
            for rp in range(2):
                bank = psum.tile([P, 512], F32, name="xt", tag="ps")
                bv = bank[:].rearrange("p (u n) -> p u n", u=2)
                for rr in range(2):
                    for u in range(2):
                        nc.tensor.transpose(bv[:, u, P * rr:P * (rr + 1)], words[:, 2 * rp + rr, 256 * g + u:256 * (g + 1):2], ident[:])
                nc.scalar.copy(out=xgw[:, 256 * rp:256 * (rp + 1), :], in_=bv.rearrange("p u n -> p n u"))

        def x_quant(b, g):
            nc.vector.quantize_mx(out=xc[:, 2 * b + g, :].bitcast(FP8X4), scales=xs[:, 2 * b + g, :], in_=xg[(b, g)][:].rearrange("p n j -> p (n j)"))

        def mm_group(out, b, r, codes, scales, c):
            for g in range(2):
                nc.tensor.matmul_mx(
                    out=out,
                    lhsT=xc[:, 2 * b + g, P * r:P * (r + 1)].bitcast(FP8X4),
                    lhsT_scale=xs[:, 2 * b + g, P * r:P * (r + 1)],
                    rhs=codes[:, 2 * c + g, :].bitcast(FP8X4),
                    rhs_scale=scales[:, 2 * c + g, :],
                    start=(g == 0),
                    stop=(g == 1),
                )

        qkb = {}
        vbb = {}

        def mm_qk(s, rp):
            c, b = divmod(s, 2)
            for rr in range(2):
                bank = psum.tile([P, 512], F32, name="qk", tag="ps")
                mm_group(bank[:], b, 2 * rp + rr, wcqk, wsqk, c)
                qkb[(s, 2 * rp + rr)] = bank

        def mm_v(s, rp):
            c, b = divmod(s, 2)
            bank = psum.tile([P, 512], F32, name="vb", tag="ps")
            bv = bank[:].rearrange("p (a n) -> p a n", a=2)
            for rr in range(2):
                mm_group(bv[:, rr, :], b, 2 * rp + rr, wcv, wsv, c)
            vbb[(s, rp)] = bank

        def mm(s):
            for rp in range(2):
                mm_qk(s, rp)
                if s < LATE_V:
                    mm_v(s, rp)

        widen(0)
        widen(1)
        cs = const.tile([P, 256], F32, name="cs")
        cs4 = cs[:].rearrange("p (r q j) -> p r q j", r=4, q=4)
        red4 = red3[:].rearrange("p (r q j) -> p r q j", r=4, q=2)
        nc.scalar.activation(out=cs4[:, :, 1:3, :], in_=red4, func=ACT.Sin)
        nc.scalar.activation(out=cs4[:, :, 0, :], in_=red4[:, :, 0, :], func=ACT.Sin)
        nc.scalar.activation(out=cs4[:, :, 3, :], in_=red4[:, :, 1, :], func=ACT.Sin, scale=-1.0)
        cs5 = cs[:].rearrange("p (r q o c) -> p r q o c", r=4, q=2, o=1)
        interleave_qk(0)
        x_turn(0, 0)
        quant_qk(0)
        interleave_qk(1)
        x_turn(0, 1)
        x_quant(0, 0)
        quant_qk(1)
        x_quant(0, 1)
        mm_qk(0, 0)
        mm_qk(0, 1)
        interleave_v(0)
        interleave_v(1)
        quant_v(0)
        quant_v(1)
        mm_v(0, 0)
        mm_v(0, 1)

        otvs = {}

        def copy_v(s, rp, engine, split):
            c, b = divmod(s, 2)
            if rp == 0:
                otvs[s] = outp.tile([P, 2, 4, HS], F32, name="otv", tag="otv")
            otv = otvs[s]
            dst = otv[:, :, 2 * rp:2 * rp + 2, :].rearrange("p h a d -> p a h d")
            src = vbb[(s, rp)][:].rearrange("p (a h d) -> p a h d", a=2, h=2)
            if engine == "v":
                nc.vector.tensor_copy(out=dst, in_=src)
            else:
                nc.scalar.copy(out=dst, in_=src)
            if split:
                nc.sync.dma_start(
                    out=out_2[b, 2 * c:2 * c + 2].rearrange("h (p r) d -> p h r d", r=4)[:, :, 2 * rp:2 * rp + 2, :].rearrange("p h r d -> p h (r d)"),
                    in_=otv[:, :, 2 * rp:2 * rp + 2, :].rearrange("p h r d -> p h (r d)"),
                )
            elif rp == 1:
                nc.sync.dma_start(
                    out=out_2[b, 2 * c:2 * c + 2].rearrange("h (p r) d -> p h (r d)", r=4),
                    in_=otv[:].rearrange("p h r d -> p h (r d)"),
                )

        for s in range(NSTEP):
            c, b = divmod(s, 2)
            otqk = outp.tile([P, 4, 4, HS], F32, name="otqk", tag="otqk")
            prod = outp.tile([P, 2, 4, 4, ROT], F32, name="prod", tag="prod")

            def rope(r):
                bv = qkb[(s, r)][:].rearrange("p (o k f) -> p o k f", o=1, k=4)
                nc.vector.tensor_tensor(
                    out=prod[:, :, :, r, :],
                    in0=bv[:, :, :, 0:ROT].to_broadcast([P, 2, 4, ROT]),
                    in1=cs5[:, r].to_broadcast([P, 2, 4, ROT]),
                    op=ALU.mult,
                )
                if r in V_COPY.get(s, ()):
                    nc.vector.tensor_copy(out=otqk[:, :, r, ROT:HS], in_=bv[:, 0, :, ROT:HS])
                else:
                    nc.scalar.copy(out=otqk[:, :, r, ROT:HS], in_=bv[:, 0, :, ROT:HS])

            def finish():
                nc.vector.tensor_tensor(
                    out=otqk[:, :, :, 0:ROT].rearrange("p k r (h j) -> p (k r) h j", h=2),
                    in0=prod[:, 0].rearrange("p k r (h j) -> p (k r) h j", h=2),
                    in1=prod[:, 1].rearrange("p k r (h j) -> p (k r) h j", h=2)[:, :, ::-1, :],
                    op=ALU.add,
                )
                for y in range(2):
                    nc.sync.dma_start(
                        out=(out_0, out_1)[y][b, 2 * c:2 * c + 2].rearrange("h (p r) d -> p h (r d)", r=4),
                        in_=otqk[:, 2 * y:2 * y + 2].rearrange("p k r d -> p k (r d)"),
                    )

            if s == 0:
                x_turn(1, 0)
                rope(0)
                x_turn(1, 1)
                rope(1)
                x_quant(1, 0)
                copy_v(0, 0, "s", False)
                rope(2)
                x_quant(1, 1)
                mm(1)
                rope(3)
                widen(2)
                finish()
                copy_v(0, 1, "s", False)
                interleave_qk(2)
                interleave_v(2)
                widen(3)
                quant_qk(2)
                quant_v(2)
                continue
            w = s + 2
            more = w < NHALF
            early_v = more and w < LATE_V
            rope(0)
            if more:
                interleave_qk(w)
            if s == LATE_V:
                interleave_v(LATE_V)
            rope(1)
            if early_v:
                interleave_v(w)
            if s == LATE_V:
                interleave_v(LATE_V + 1)
            if s < LATE_V:
                copy_v(s, 0, "s", False)
            if more:
                quant_qk(w)
            if s == LATE_V:
                quant_v(LATE_V)
            rope(2)
            if early_v:
                quant_v(w)
            if s + 1 < NSTEP:
                mm(s + 1)
            rope(3)
            if s == LATE_V:
                quant_v(LATE_V + 1)
            if s + 3 < NHALF:
                widen(s + 3)
            finish()
            if s < LATE_V:
                copy_v(s, 1, "s", False)

        for s in range(LATE_V, NSTEP):
            for rp in range(2):
                mm_v(s, rp)
        copy_v(LATE_V, 0, "s", False)
        copy_v(LATE_V, 1, "v", False)
        copy_v(LATE_V + 1, 0, "s", True)
        copy_v(LATE_V + 1, 1, "v", True)
